import numpy as np
import ml_dtypes


def mxq(x, axis, fmt="e4m3"):
    dtype, down = {"e4m3": (ml_dtypes.float8_e4m3fn, 7), "e5m2": (ml_dtypes.float8_e5m2, 14)}[fmt]
    v = np.moveaxis(np.asarray(x, np.float32).astype(ml_dtypes.bfloat16).astype(np.float64), axis, -1)
    blocks = v.reshape(v.shape[:-1] + (-1, 32))
    amax = np.abs(blocks).max(-1, keepdims=True)
    byte = np.maximum(np.where(amax > 0, np.frexp(amax)[1] - 1 + 127, 0) - down, 1)
    scale = np.exp2(byte - 127.0)
    codes = (blocks / scale).astype(np.float32).astype(dtype).astype(np.float64)
    return np.moveaxis((codes * scale).reshape(v.shape), -1, axis)


WIDE = False


def mx_kscale(k):
    if not WIDE:
        return np.ones(k)
    levels = np.array([10, -10, 5, -5, 0])
    if k % 512:
        return np.exp2(np.random.permutation(np.resize(levels, k // 32))).repeat(32)
    a = np.empty((k // 512, 16))
    for p in range(k // 512):
        a[p, :8] = np.random.permutation(np.resize(levels, 8))
        for g in range(8):
            far = levels[np.abs(levels - a[p, g]) >= 10]
            a[p, g + 8] = far[np.random.randint(len(far))]
    return np.exp2(a.ravel()).repeat(32)


BF16 = ml_dtypes.bfloat16


def bf(x):
    return np.asarray(x, np.float32).astype(BF16)


def f64(x):
    return np.asarray(x).astype(np.float64)


B, I, C, L, O, KW, P = 2, 1024, 2, 2048, 128, 3, 1


def draw0():
    s = mx_kscale(I)
    return {"x": bf(np.random.standard_normal((B, I, C, L)) * s[None, :, None, None]),
            "time_tensor": bf(np.random.uniform(0.0, 1.0, (B, C, L))),
            "weights": bf(np.random.standard_normal((O, I, C, KW)) / np.sqrt(I * KW) / s[None, :, None, None])}


def core(x, time_tensor, weights):
    xq = mxq(f64(x).transpose(0, 2, 1, 3), 2, "e4m3")
    wt = f64(weights).transpose(3, 2, 0, 1)
    tp = np.pad(f64(time_tensor), ((0, 0), (0, 0), (P, P)))
    Lw = L + 2 * P - KW + 1
    conv = np.zeros((B, C, O, Lw))
    for j in range(KW):
        y = mxq(wt[j], 2, "e4m3") @ xq
        conv = conv + np.pad(y, ((0, 0), (0, 0), (0, 0), (P, P)))[..., j:j + Lw]
    conv = np.transpose(conv, (0, 2, 1, 3))
    conv = np.pad(conv, ((0, 0), (0, 0), (0, 0), (P, P)))
    out = conv * tp[:, None, :, :]
    return out[..., P:-P]


def e4m3fn_bytes(y):
    return np.clip(np.asarray(y, np.float64), -448.0, 448.0).astype(np.float32).astype(ml_dtypes.float8_e4m3fn).view(np.uint8)


def e4m3fn_values(b):
    return np.asarray(b, np.uint8).view(ml_dtypes.float8_e4m3fn).astype(np.float64)


def setup_inputs():
    d = draw0()
    x0 = np.asarray(d['x']).astype(np.float64)
    s = (np.max(np.abs(x0), axis=(0, 2, 3), keepdims=True) / 448.0).astype(np.float32)
    out = {}
    for k, v in d.items():
        if k == 'x':
            out['x_bytes'] = e4m3fn_bytes(x0 / s.astype(np.float64))
            out['x_scale'] = s
        else:
            out[k] = v
    return out


def reference(x_bytes, x_scale, time_tensor, weights):
    return core(e4m3fn_values(x_bytes) * x_scale.astype(np.float64), time_tensor, weights)

@@ -1,0 +1,193 @@
+from contextlib import ExitStack
+
+import concourse.mybir as mybir
+from concourse.masks import make_identity
+
+B, I, C, L, O, KW = 2, 1024, 2, 2048, 128, 3
+FLOPS = 2 * B * C * O * I * KW * L
+
+F32 = mybir.dt.float32
+BF16 = mybir.dt.bfloat16
+I32 = mybir.dt.int32
+U8 = mybir.dt.uint8
+FP8 = mybir.dt.float8_e4m3fn
+FP8X4 = mybir.dt.float8_e4m3fn_x4
+COPY = mybir.ActivationFunctionType.Copy
+MULT = mybir.AluOpType.mult
+
+P = 128
+G = 2
+T = 4
+R = 4
+Q = L // R
+WIN = 128
+
+PADW, PITCHW = 16, 546
+PADB, PITCHB = 64, 642
+E4W, EM1W = PADW, PITCHW + PADW - 2
+E4B, EM1B = PADB, PITCHB + PADB - 2
+
+ROWS = [(0, 0), (1, 0), (0, 1), (1, 1)]
+PIECES = [
+    [(0, 128), (128, 128), (256, 256)],
+    [(0, 256), (256, 256)],
+    [(0, 256), (256, 256)],
+    [(0, 256), (256, 128), (384, 128)],
+]
+
+
+def tile_timeawareconv1d_t_kernel(tc, x_bytes, x_scale, time_tensor, weights, out):
+    nc = tc.nc
+    with ExitStack() as ctx:
+        keep = ctx.enter_context(tc.tile_pool(name="keep", bufs=1))
+        wdpool = ctx.enter_context(tc.tile_pool(name="wdpool", bufs=4))
+        gqpool = ctx.enter_context(tc.tile_pool(name="gqpool", bufs=3))
+        opool = ctx.enter_context(tc.tile_pool(name="opool", bufs=4))
+        pwpool = ctx.enter_context(tc.psum_pool(name="pwpool", bufs=2))
+        popool = ctx.enter_context(tc.psum_pool(name="popool", bufs=6))
+
+        ident = keep.tile([P, P], BF16, name="ident")
+        make_identity(nc, ident[:])
+        sc = keep.tile([P, G, T], F32, name="sc")
+        tt = keep.tile([P, B * C * L], BF16, name="tt")
+        w_raw = [keep.tile([P, 512 * C * KW], BF16, name="w_raw%d" % g) for g in range(G)]
+        w_codes = keep.tile([P, C * KW * G * P], I32, name="w_codes", align_bytes=64)
+        w_plane = keep.tile([P, C * KW * G * P], U8, name="w_plane", align_bytes=64)
+        xb = [keep.tile([P, G, T, L], U8, name="xbytes%d" % i) for i in range(4)]
+        codes = [[keep.tile([P, R * Q], I32, name="codes%d_%d" % (s, g), align_bytes=64) for g in range(G)] for s in range(2)]
+        plane = [[keep.tile([P, R * Q], U8, name="plane%d_%d" % (s, g), align_bytes=64) for g in range(G)] for s in range(2)]
+        xcodes = [[keep.tile([P, 2 * PITCHW], I32, name="xcodes%d_%d" % (s, g), align_bytes=64) for g in range(G)] for s in range(2)]
+        xplane = [[keep.tile([P, 2 * PITCHB], U8, name="xplane%d_%d" % (s, g), align_bytes=64) for g in range(G)] for s in range(2)]
+
+        def load_x(row, g, l0, l1):
+            b, c = ROWS[row]
+            src = x_bytes[b].rearrange("(g p t) c l -> g p t c l", g=G, p=P, t=T)
+            nc.sync.dma_start(out=xb[row][:, g, :, l0:l1], in_=src[g][:, :, c, l0:l1])
+
+        nc.sync.dma_start(out=sc[:], in_=x_scale.rearrange("o (g p t) a b -> p (o g) (t a b)", g=G, p=P, t=T))
+        for g in range(G):
+            load_x(0, g, 0, 512)
+        for g in range(G):
+            nc.sync.dma_start(out=w_raw[g][:], in_=weights[:, g * 512:(g + 1) * 512, :, :].rearrange("o i c j -> o (i c j)"))
+        for g in range(G):
+            load_x(0, g, 512, L)
+        nc.sync.dma_start(out=tt[:], in_=time_tensor.rearrange("b c l -> (b c l)").partition_broadcast(P))
+        for row in range(1, 4):
+            for g in range(G):
+                load_x(row, g, 0, L)
+
+        for s in range(2):
+            for g in range(G):
+                nc.vector.memset(xcodes[s][g][:], 0)
+                nc.vector.memset(xplane[s][g][:].bitcast(I32), 0)
+                nc.vector.memset(plane[s][g][:].bitcast(I32), 0)
+
+        def prep_weights(c):
+            wg = gqpool.tile([P, KW * G * 512], BF16, name="wg", tag="gq", align_bytes=64)
+            for j in range(KW):
+                for g in range(G):
+                    k = j * G + g
+                    pw = pwpool.tile([P, T, P], BF16, name="pw")
+                    view = w_raw[g][:].rearrange("o (p t c j) -> o p t c j", p=P, t=T, c=C, j=KW)
+                    for t in range(T):
+                        nc.tensor.transpose(out=pw[:, t, :], in_=view[:, :, t, c, j], identity=ident[:])
+                    nc.scalar.copy(out=wg[:, k * 512:(k + 1) * 512].rearrange("p (o t) -> p o t", t=T),
+                                   in_=pw[:].rearrange("p t o -> p o t"))
+            base = c * KW * G * P
+            for a, n in ((0, 512), (512, 256)):
+                nc.vector.quantize_mx(out=w_codes[:, base + a:base + a + n].bitcast(FP8X4),
+                                      scales=w_plane[:, base + a:base + a + n],
+                                      in_=wg[:, 4 * a:4 * (a + n)])
+
+        def widen(row, q0, nq):
+            tiles = []
+            for g in range(G):
+                wd = wdpool.tile([P, T, R * nq], BF16, name="wd")
+                for t in range(T):
+                    nc.scalar.activation(out=wd[:, t, :], in_=xb[row][:, g, t, R * q0:R * (q0 + nq)].bitcast(FP8),
+                                         func=COPY, scale=sc[:, g, t:t + 1])
+                tiles.append(wd)
+            return tiles
+
+        def interleave(wds, nq):
+            tiles = []
+            for g in range(G):
+                gq = gqpool.tile([P, R * nq * T], BF16, name="gq", tag="gq", align_bytes=64)
+                nc.vector.tensor_copy(out=gq[:].rearrange("p (r q t) -> p r q t", r=R, t=T),
+                                      in_=wds[g][:].rearrange("p t (q r) -> p r q t", r=R))
+                tiles.append(gq)
+            return tiles
+
+        def quantise(s, gqs, q0, nq):
+            for g in range(G):
+                nc.vector.quantize_mx(out=codes[s][g][:, R * q0:R * (q0 + nq)].bitcast(FP8X4),
+                                      scales=plane[s][g][:, R * q0:R * (q0 + nq)],
+                                      in_=gqs[g][:])
+
+        def shift(s, q0, nq):
+            for g in range(G):
+                nc.vector.tensor_copy(
+                    out=xcodes[s][g][:].rearrange("p (e w) -> p e w", e=2)[:, :, PADW + q0 - 1:PADW + q0 - 1 + nq],
+                    in_=codes[s][g][:, R * q0:R * (q0 + nq)].rearrange("p (r q) -> p r q", r=R)[:, 0:R:R - 1, :])
+                nc.vector.tensor_copy(
+                    out=xplane[s][g][:].rearrange("p (e w) -> p e w", e=2)[:, :, PADB + q0 - 1:PADB + q0 - 1 + nq],
+                    in_=plane[s][g][:, R * q0:R * (q0 + nq)].rearrange("p (r q) -> p r q", r=R)[:, 0:R:R - 1, :])
+
+        def operand(row, s, g, cls, w):
+            if cls < 0:
+                return (xcodes[s][g][:, EM1W + WIN * w:EM1W + WIN * (w + 1)], xplane[s][g][:, EM1B + WIN * w:EM1B + WIN * (w + 1)])
+            if cls >= R:
+                return (xcodes[s][g][:, E4W + WIN * w:E4W + WIN * (w + 1)], xplane[s][g][:, E4B + WIN * w:E4B + WIN * (w + 1)])
+            for q0, nq in PIECES[row]:
+                if q0 <= WIN * w < q0 + nq:
+                    a = R * q0 + cls * nq + WIN * w - q0
+                    return (codes[s][g][:, a:a + WIN], plane[s][g][:, a:a + WIN])
+            raise ValueError("no piece")
+
+        def multiply(row, w):
+            b, c = ROWS[row]
+            s = row % 2
+            po = popool.tile([P, R * WIN], F32, name="po")
+            for r in range(R):
+                k = 0
+                for g in range(G):
+                    for j in range(KW):
+                        rhs, rhs_scale = operand(row, s, g, r + j - 1, w)
+                        a = ((c * KW + j) * G + g) * P
+                        nc.tensor.matmul_mx(out=po[:, r * WIN:(r + 1) * WIN],
+                                            lhsT=w_codes[:, a:a + P].bitcast(FP8X4), lhsT_scale=w_plane[:, a:a + P],
+                                            rhs=rhs.bitcast(FP8X4), rhs_scale=rhs_scale,
+                                            start=(k == 0), stop=(k == G * KW - 1))
+                        k += 1
+            return po
+
+        def finish(row, w, po):
+            b, c = ROWS[row]
+            l0 = R * WIN * w
+            t0 = (b * C + c) * L + l0
+            osb = opool.tile([P, R * WIN], F32, name="osb")
+            nc.vector.tensor_tensor(out=osb[:].rearrange("p (q r) -> p q r", r=R),
+                                    in0=po[:].rearrange("p (r q) -> p q r", r=R),
+                                    in1=tt[:, t0:t0 + R * WIN].rearrange("p (q r) -> p q r", r=R), op=MULT)
+            nc.sync.dma_start(out=out[b, :, c, l0:l0 + R * WIN], in_=osb[:])
+
+        flat = [(row, q0, nq) for row in range(4) for (q0, nq) in PIECES[row]]
+        wds = {0: widen(*flat[0])}
+        prep_weights(0)
+        pending = []
+        for n, (row, q0, nq) in enumerate(flat):
+            if n + 1 < len(flat):
+                wds[n + 1] = widen(*flat[n + 1])
+            if n == 4:
+                prep_weights(1)
+            gqs = interleave(wds[n], nq)
+            quantise(row % 2, gqs, q0, nq)
+            shift(row % 2, q0, nq)
+            first = max(q0 // WIN - 1, 0)
+            last = (q0 + nq) // WIN - 1 if q0 + nq < Q else Q // WIN
+            ready = [(row, w, multiply(row, w)) for w in range(first, last)]
+            for item in pending:
+                finish(*item)
+            pending = ready
+        for item in pending:
+            finish(*item)

@@ -34,13 +34,15 @@ PIECES = [
     [(0, 256), (256, 256)],
     [(0, 256), (256, 128), (384, 128)],
 ]
+DMA_SHIFT = False
+V_WIDENS = ((0, 1),)
 
 
 def tile_timeawareconv1d_t_kernel(tc, x_bytes, x_scale, time_tensor, weights, out):
     nc = tc.nc
     with ExitStack() as ctx:
         keep = ctx.enter_context(tc.tile_pool(name="keep", bufs=1))
-        wdpool = ctx.enter_context(tc.tile_pool(name="wdpool", bufs=4))
+        wdpool = ctx.enter_context(tc.tile_pool(name="wdpool", bufs=5))
         gqpool = ctx.enter_context(tc.tile_pool(name="gqpool", bufs=3))
         opool = ctx.enter_context(tc.tile_pool(name="opool", bufs=4))
         pwpool = ctx.enter_context(tc.psum_pool(name="pwpool", bufs=2))
@@ -55,9 +57,9 @@ def tile_timeawareconv1d_t_kernel(tc, x_bytes, x_scale, time_tensor, weights, ou
         w_plane = keep.tile([P, C * KW * G * P], U8, name="w_plane", align_bytes=64)
         xb = [keep.tile([P, G, T, L], U8, name="xbytes%d" % i) for i in range(4)]
         codes = [[keep.tile([P, R * Q], I32, name="codes%d_%d" % (s, g), align_bytes=64) for g in range(G)] for s in range(2)]
-        plane = [[keep.tile([P, R * Q], U8, name="plane%d_%d" % (s, g), align_bytes=64) for g in range(G)] for s in range(2)]
         xcodes = [[keep.tile([P, 2 * PITCHW], I32, name="xcodes%d_%d" % (s, g), align_bytes=64) for g in range(G)] for s in range(2)]
-        xplane = [[keep.tile([P, 2 * PITCHB], U8, name="xplane%d_%d" % (s, g), align_bytes=64) for g in range(G)] for s in range(2)]
+        plane = [keep.tile([P, R * Q], U8, name="plane%d" % s, align_bytes=64) for s in range(2)]
+        xplane = [keep.tile([P, 2 * PITCHB], U8, name="xplane%d" % s, align_bytes=64) for s in range(2)]
 
         def load_x(row, g, l0, l1):
             b, c = ROWS[row]
@@ -77,10 +79,10 @@ def tile_timeawareconv1d_t_kernel(tc, x_bytes, x_scale, time_tensor, weights, ou
                 load_x(row, g, 0, L)
 
         for s in range(2):
+            nc.vector.memset(plane[s][:].bitcast(I32), 0)
+            nc.vector.memset(xplane[s][:].bitcast(I32), 0)
             for g in range(G):
                 nc.vector.memset(xcodes[s][g][:], 0)
-                nc.vector.memset(xplane[s][g][:].bitcast(I32), 0)
-                nc.vector.memset(plane[s][g][:].bitcast(I32), 0)
 
         def prep_weights(c):
             wg = gqpool.tile([P, KW * G * 512], BF16, name="wg", tag="gq", align_bytes=64)
@@ -99,13 +101,16 @@ def tile_timeawareconv1d_t_kernel(tc, x_bytes, x_scale, time_tensor, weights, ou
                                       scales=w_plane[:, base + a:base + a + n],
                                       in_=wg[:, 4 * a:4 * (a + n)])
 
-        def widen(row, q0, nq):
+        def widen(n, row, q0, nq):
             tiles = []
             for g in range(G):
-                wd = wdpool.tile([P, T, R * nq], BF16, name="wd")
+                wd = wdpool.tile([P, T, R * nq], BF16, name="wd", tag="wd")
                 for t in range(T):
-                    nc.scalar.activation(out=wd[:, t, :], in_=xb[row][:, g, t, R * q0:R * (q0 + nq)].bitcast(FP8),
-                                         func=COPY, scale=sc[:, g, t:t + 1])
+                    src = xb[row][:, g, t, R * q0:R * (q0 + nq)].bitcast(FP8)
+                    if (n, g) in V_WIDENS:
+                        nc.vector.tensor_scalar(out=wd[:, t, :], in0=src, scalar1=sc[:, g, t:t + 1], scalar2=None, op0=MULT)
+                    else:
+                        nc.scalar.activation(out=wd[:, t, :], in_=src, func=COPY, scale=sc[:, g, t:t + 1])
                 tiles.append(wd)
             return tiles
 
@@ -113,42 +118,53 @@ def tile_timeawareconv1d_t_kernel(tc, x_bytes, x_scale, time_tensor, weights, ou
             tiles = []
             for g in range(G):
                 gq = gqpool.tile([P, R * nq * T], BF16, name="gq", tag="gq", align_bytes=64)
-                nc.vector.tensor_copy(out=gq[:].rearrange("p (r q t) -> p r q t", r=R, t=T),
-                                      in_=wds[g][:].rearrange("p t (q r) -> p r q t", r=R))
+                nc.vector.tensor_copy(out=gq[:].rearrange("p (r q t) -> p q t r", r=R, t=T),
+                                      in_=wds[g][:].rearrange("p t (q r) -> p q t r", r=R))
                 tiles.append(gq)
             return tiles
 
         def quantise(s, gqs, q0, nq):
-            for g in range(G):
-                nc.vector.quantize_mx(out=codes[s][g][:, R * q0:R * (q0 + nq)].bitcast(FP8X4),
-                                      scales=plane[s][g][:, R * q0:R * (q0 + nq)],
-                                      in_=gqs[g][:])
+            a, n = R * q0, R * nq
+            nc.vector.quantize_mx(out=codes[s][0][:, a:a + n].bitcast(FP8X4), scales=plane[s][:, a:a + n], in_=gqs[0][:])
+            step = min(n, 512)
+            for h in range(0, n, step):
+                nc.vector.quantize_mx(out=codes[s][1][:, a + h:a + h + step].bitcast(FP8X4),
+                                      scales=plane[s][4:P, a + h:a + h + step],
+                                      in_=gqs[1][:, T * h:T * (h + step)])
 
-        def shift(s, q0, nq):
+        def shift(s, q0, nq, by_dma):
             for g in range(G):
-                nc.vector.tensor_copy(
-                    out=xcodes[s][g][:].rearrange("p (e w) -> p e w", e=2)[:, :, PADW + q0 - 1:PADW + q0 - 1 + nq],
-                    in_=codes[s][g][:, R * q0:R * (q0 + nq)].rearrange("p (r q) -> p r q", r=R)[:, 0:R:R - 1, :])
-                nc.vector.tensor_copy(
-                    out=xplane[s][g][:].rearrange("p (e w) -> p e w", e=2)[:, :, PADB + q0 - 1:PADB + q0 - 1 + nq],
-                    in_=plane[s][g][:, R * q0:R * (q0 + nq)].rearrange("p (r q) -> p r q", r=R)[:, 0:R:R - 1, :])
+                dst = xcodes[s][g][:].rearrange("p (e w) -> p e w", e=2)[:, :, PADW + q0 - 1:PADW + q0 - 1 + nq]
+                src = codes[s][g][:, R * q0:R * (q0 + nq)].rearrange("p (r q) -> p r q", r=R)[:, 0:R:R - 1, :]
+                if by_dma:
+                    nc.sync.dma_start(out=dst, in_=src)
+                else:
+                    nc.vector.tensor_copy(out=dst, in_=src)
+            nc.vector.tensor_copy(
+                out=xplane[s][:].rearrange("p (e w) -> p e w", e=2)[:, :, PADB + q0 - 1:PADB + q0 - 1 + nq],
+                in_=plane[s][:, R * q0:R * (q0 + nq)].rearrange("p (r q) -> p r q", r=R)[:, 0:R:R - 1, :])
 
         def operand(row, s, g, cls, w):
+            k = 4 * g
             if cls < 0:
-                return (xcodes[s][g][:, EM1W + WIN * w:EM1W + WIN * (w + 1)], xplane[s][g][:, EM1B + WIN * w:EM1B + WIN * (w + 1)])
+                return (xcodes[s][g][:, EM1W + WIN * w:EM1W + WIN * (w + 1)], xplane[s][k:P, EM1B + WIN * w:EM1B + WIN * (w + 1)])
             if cls >= R:
-                return (xcodes[s][g][:, E4W + WIN * w:E4W + WIN * (w + 1)], xplane[s][g][:, E4B + WIN * w:E4B + WIN * (w + 1)])
+                return (xcodes[s][g][:, E4W + WIN * w:E4W + WIN * (w + 1)], xplane[s][k:P, E4B + WIN * w:E4B + WIN * (w + 1)])
             for q0, nq in PIECES[row]:
                 if q0 <= WIN * w < q0 + nq:
                     a = R * q0 + cls * nq + WIN * w - q0
-                    return (codes[s][g][:, a:a + WIN], plane[s][g][:, a:a + WIN])
+                    return (codes[s][g][:, a:a + WIN], plane[s][k:P, a:a + WIN])
             raise ValueError("no piece")
 
-        def multiply(row, w):
+        banks = {}
+
+        def multiply(row, w, classes):
             b, c = ROWS[row]
             s = row % 2
-            po = popool.tile([P, R * WIN], F32, name="po")
-            for r in range(R):
+            if (row, w) not in banks:
+                banks[(row, w)] = popool.tile([P, R * WIN], F32, name="po", tag="po")
+            po = banks[(row, w)]
+            for r in classes:
                 k = 0
                 for g in range(G):
                     for j in range(KW):
@@ -159,35 +175,43 @@ def tile_timeawareconv1d_t_kernel(tc, x_bytes, x_scale, time_tensor, weights, ou
                                             rhs=rhs.bitcast(FP8X4), rhs_scale=rhs_scale,
                                             start=(k == 0), stop=(k == G * KW - 1))
                         k += 1
-            return po
 
-        def finish(row, w, po):
+        def finish(row, w):
             b, c = ROWS[row]
+            po = banks[(row, w)]
             l0 = R * WIN * w
             t0 = (b * C + c) * L + l0
-            osb = opool.tile([P, R * WIN], F32, name="osb")
+            osb = opool.tile([P, R * WIN], F32, name="osb", tag="osb")
             nc.vector.tensor_tensor(out=osb[:].rearrange("p (q r) -> p q r", r=R),
                                     in0=po[:].rearrange("p (r q) -> p q r", r=R),
                                     in1=tt[:, t0:t0 + R * WIN].rearrange("p (q r) -> p q r", r=R), op=MULT)
             nc.sync.dma_start(out=out[b, :, c, l0:l0 + R * WIN], in_=osb[:])
 
         flat = [(row, q0, nq) for row in range(4) for (q0, nq) in PIECES[row]]
-        wds = {0: widen(*flat[0])}
+        wds = {0: widen(0, *flat[0])}
         prep_weights(0)
         pending = []
         for n, (row, q0, nq) in enumerate(flat):
             if n + 1 < len(flat):
-                wds[n + 1] = widen(*flat[n + 1])
+                wds[n + 1] = widen(n + 1, *flat[n + 1])
             if n == 4:
                 prep_weights(1)
             gqs = interleave(wds[n], nq)
             quantise(row % 2, gqs, q0, nq)
-            shift(row % 2, q0, nq)
-            first = max(q0 // WIN - 1, 0)
-            last = (q0 + nq) // WIN - 1 if q0 + nq < Q else Q // WIN
-            ready = [(row, w, multiply(row, w)) for w in range(first, last)]
             for item in pending:
                 finish(*item)
-            pending = ready
+            shift(row % 2, q0, nq, DMA_SHIFT and n + 2 < len(flat))
+            w0, w1 = q0 // WIN, (q0 + nq) // WIN
+            done = []
+            for w in range(w0, w1):
+                multiply(row, w, (1, 2))
+            if w0 > 0:
+                multiply(row, w0 - 1, (3,))
+                done.append((row, w0 - 1))
+            for w in range(w0, w1):
+                multiply(row, w, (0, 3) if (w + 1 < w1 or w1 * WIN == Q) else (0,))
+                if w + 1 < w1 or w1 * WIN == Q:
+                    done.append((row, w))
+            pending = done
         for item in pending:
             finish(*item)

@@ -34,8 +34,10 @@ PIECES = [
     [(0, 256), (256, 256)],
     [(0, 256), (256, 128), (384, 128)],
 ]
-DMA_SHIFT = False
-V_WIDENS = ((0, 1),)
+V_WIDENS = ((0, 1), (1, 1), (2, 1))
+S_SHARE = 1 / 8
+S_SHARE_TAIL = 3 / 8
+MANUAL = False
 
 
 def tile_timeawareconv1d_t_kernel(tc, x_bytes, x_scale, time_tensor, weights, out):
@@ -66,17 +68,25 @@ def tile_timeawareconv1d_t_kernel(tc, x_bytes, x_scale, time_tensor, weights, ou
             src = x_bytes[b].rearrange("(g p t) c l -> g p t c l", g=G, p=P, t=T)
             nc.sync.dma_start(out=xb[row][:, g, :, l0:l1], in_=src[g][:, :, c, l0:l1])
 
+        def load_time(row):
+            b, c = ROWS[row]
+            t0 = (b * C + c) * L
+            nc.sync.dma_start(out=tt[:, t0:t0 + L], in_=time_tensor[b, c].partition_broadcast(P))
+
         nc.sync.dma_start(out=sc[:], in_=x_scale.rearrange("o (g p t) a b -> p (o g) (t a b)", g=G, p=P, t=T))
+        for q0, nq in PIECES[0]:
+            for g in range(G):
+                load_x(0, g, R * q0, R * (q0 + nq))
         for g in range(G):
-            load_x(0, g, 0, 512)
+            load_x(1, g, 0, L)
         for g in range(G):
             nc.sync.dma_start(out=w_raw[g][:], in_=weights[:, g * 512:(g + 1) * 512, :, :].rearrange("o i c j -> o (i c j)"))
-        for g in range(G):
-            load_x(0, g, 512, L)
-        nc.sync.dma_start(out=tt[:], in_=time_tensor.rearrange("b c l -> (b c l)").partition_broadcast(P))
-        for row in range(1, 4):
+        load_time(0)
+        for row in range(2, 4):
             for g in range(G):
                 load_x(row, g, 0, L)
+            load_time(row - 1)
+        load_time(3)
 
         for s in range(2):
             nc.vector.memset(plane[s][:].bitcast(I32), 0)
@@ -84,17 +94,24 @@ def tile_timeawareconv1d_t_kernel(tc, x_bytes, x_scale, time_tensor, weights, ou
             for g in range(G):
                 nc.vector.memset(xcodes[s][g][:], 0)
 
-        def prep_weights(c):
+        if MANUAL:
+            ctx.enter_context(tc.manual_schedule(engines={mybir.EngineType.Activation, mybir.EngineType.DVE}))
+
+        def transpose_weights(c):
+            tiles = []
             wg = gqpool.tile([P, KW * G * 512], BF16, name="wg", tag="gq", align_bytes=64)
             for j in range(KW):
                 for g in range(G):
                     k = j * G + g
-                    pw = pwpool.tile([P, T, P], BF16, name="pw")
+                    pw = pwpool.tile([P, T, P], BF16, name="pw", tag="pw")
                     view = w_raw[g][:].rearrange("o (p t c j) -> o p t c j", p=P, t=T, c=C, j=KW)
                     for t in range(T):
                         nc.tensor.transpose(out=pw[:, t, :], in_=view[:, :, t, c, j], identity=ident[:])
                     nc.scalar.copy(out=wg[:, k * 512:(k + 1) * 512].rearrange("p (o t) -> p o t", t=T),
                                    in_=pw[:].rearrange("p t o -> p o t"))
+            return wg
+
+        def quantise_weights(c, wg):
             base = c * KW * G * P
             for a, n in ((0, 512), (512, 256)):
                 nc.vector.quantize_mx(out=w_codes[:, base + a:base + a + n].bitcast(FP8X4),
@@ -114,32 +131,35 @@ def tile_timeawareconv1d_t_kernel(tc, x_bytes, x_scale, time_tensor, weights, ou
                 tiles.append(wd)
             return tiles
 
-        def interleave(wds, nq):
+        def interleave(wds, nq, share):
             tiles = []
+            cut = nq - 4 * int(nq * share / 4)
             for g in range(G):
                 gq = gqpool.tile([P, R * nq * T], BF16, name="gq", tag="gq", align_bytes=64)
-                nc.vector.tensor_copy(out=gq[:].rearrange("p (r q t) -> p q t r", r=R, t=T),
-                                      in_=wds[g][:].rearrange("p t (q r) -> p q t r", r=R))
+                dst = gq[:].rearrange("p (r q t) -> p q t r", r=R, t=T)
+                src = wds[g][:].rearrange("p t (q r) -> p q t r", r=R)
+                if cut < nq:
+                    nc.scalar.copy(out=dst[:, cut:nq], in_=src[:, cut:nq])
+                nc.vector.tensor_copy(out=dst[:, 0:cut], in_=src[:, 0:cut])
                 tiles.append(gq)
             return tiles
 
-        def quantise(s, gqs, q0, nq):
+        def quantise(s, g, gqs, q0, nq):
             a, n = R * q0, R * nq
-            nc.vector.quantize_mx(out=codes[s][0][:, a:a + n].bitcast(FP8X4), scales=plane[s][:, a:a + n], in_=gqs[0][:])
-            step = min(n, 512)
-            for h in range(0, n, step):
-                nc.vector.quantize_mx(out=codes[s][1][:, a + h:a + h + step].bitcast(FP8X4),
-                                      scales=plane[s][4:P, a + h:a + h + step],
-                                      in_=gqs[1][:, T * h:T * (h + step)])
+            if g == 0:
+                nc.vector.quantize_mx(out=codes[s][0][:, a:a + n].bitcast(FP8X4), scales=plane[s][:, a:a + n], in_=gqs[0][:])
+            else:
+                step = min(n, 512)
+                for h in range(0, n, step):
+                    nc.vector.quantize_mx(out=codes[s][1][:, a + h:a + h + step].bitcast(FP8X4),
+                                          scales=plane[s][4:P, a + h:a + h + step],
+                                          in_=gqs[1][:, T * h:T * (h + step)])
 
-        def shift(s, q0, nq, by_dma):
+        def shift(s, q0, nq):
             for g in range(G):
-                dst = xcodes[s][g][:].rearrange("p (e w) -> p e w", e=2)[:, :, PADW + q0 - 1:PADW + q0 - 1 + nq]
-                src = codes[s][g][:, R * q0:R * (q0 + nq)].rearrange("p (r q) -> p r q", r=R)[:, 0:R:R - 1, :]
-                if by_dma:
-                    nc.sync.dma_start(out=dst, in_=src)
-                else:
-                    nc.vector.tensor_copy(out=dst, in_=src)
+                nc.vector.tensor_copy(
+                    out=xcodes[s][g][:].rearrange("p (e w) -> p e w", e=2)[:, :, PADW + q0 - 1:PADW + q0 - 1 + nq],
+                    in_=codes[s][g][:, R * q0:R * (q0 + nq)].rearrange("p (r q) -> p r q", r=R)[:, 0:R:R - 1, :])
             nc.vector.tensor_copy(
                 out=xplane[s][:].rearrange("p (e w) -> p e w", e=2)[:, :, PADB + q0 - 1:PADB + q0 - 1 + nq],
                 in_=plane[s][:, R * q0:R * (q0 + nq)].rearrange("p (r q) -> p r q", r=R)[:, 0:R:R - 1, :])
@@ -188,30 +208,44 @@ def tile_timeawareconv1d_t_kernel(tc, x_bytes, x_scale, time_tensor, weights, ou
             nc.sync.dma_start(out=out[b, :, c, l0:l0 + R * WIN], in_=osb[:])
 
         flat = [(row, q0, nq) for row in range(4) for (q0, nq) in PIECES[row]]
+        last = len(flat) - 1
+        w_steps = {2: 0, 4: 1}
         wds = {0: widen(0, *flat[0])}
-        prep_weights(0)
         pending = []
+        backlog = []
+        wg = None
         for n, (row, q0, nq) in enumerate(flat):
-            if n + 1 < len(flat):
+            gqs = interleave(wds[n], nq, S_SHARE_TAIL if n + 2 > last else S_SHARE)
+            if n < last:
                 wds[n + 1] = widen(n + 1, *flat[n + 1])
-            if n == 4:
-                prep_weights(1)
-            gqs = interleave(wds[n], nq)
-            quantise(row % 2, gqs, q0, nq)
-            for item in pending:
+            if n in w_steps:
+                wg = transpose_weights(w_steps[n])
+            quantise(row % 2, 0, gqs, q0, nq)
+            for item in pending[:1]:
                 finish(*item)
-            shift(row % 2, q0, nq, DMA_SHIFT and n + 2 < len(flat))
+            quantise(row % 2, 1, gqs, q0, nq)
+            for item in pending[1:]:
+                finish(*item)
+            if n in w_steps:
+                quantise_weights(w_steps[n], wg)
+            shift(row % 2, q0, nq)
             w0, w1 = q0 // WIN, (q0 + nq) // WIN
-            done = []
+            whole = w1 * WIN == Q
             for w in range(w0, w1):
-                multiply(row, w, (1, 2))
+                backlog.append((row, w, (1, 2), False))
             if w0 > 0:
-                multiply(row, w0 - 1, (3,))
-                done.append((row, w0 - 1))
+                backlog.append((row, w0 - 1, (3,), True))
             for w in range(w0, w1):
-                multiply(row, w, (0, 3) if (w + 1 < w1 or w1 * WIN == Q) else (0,))
-                if w + 1 < w1 or w1 * WIN == Q:
-                    done.append((row, w))
-            pending = done
+                if w + 1 < w1 or whole:
+                    backlog.append((row, w, (0, 3), True))
+                else:
+                    backlog.append((row, w, (0,), False))
+            pending = []
+            if n >= 2:
+                for brow, bw, classes, closes in backlog:
+                    multiply(brow, bw, classes)
+                    if closes:
+                        pending.append((brow, bw))
+                backlog = []
         for item in pending:
             finish(*item)

@@ -22,9 +22,9 @@ R = 4
 Q = L // R
 WIN = 128
 
-PADW, PITCHW = 16, 546
+C0, C3, C12 = 0, Q, 2 * Q
+E4W, EM1W = 0, Q
 PADB, PITCHB = 64, 642
-E4W, EM1W = PADW, PITCHW + PADW - 2
 E4B, EM1B = PADB, PITCHB + PADB - 2
 
 ROWS = [(0, 0), (1, 0), (0, 1), (1, 1)]
@@ -35,9 +35,9 @@ PIECES = [
     [(0, 256), (256, 128), (384, 128)],
 ]
 V_WIDENS = ((0, 1), (1, 1), (2, 1))
-S_SHARE = 1 / 8
-S_SHARE_TAIL = 3 / 8
-MANUAL = False
+S_SHARE = 1 / 16
+S_SHARE_TAIL = 1 / 4
+V_SHIFTS = 2
 
 
 def tile_timeawareconv1d_t_kernel(tc, x_bytes, x_scale, time_tensor, weights, out):
@@ -58,8 +58,8 @@ def tile_timeawareconv1d_t_kernel(tc, x_bytes, x_scale, time_tensor, weights, ou
         w_codes = keep.tile([P, C * KW * G * P], I32, name="w_codes", align_bytes=64)
         w_plane = keep.tile([P, C * KW * G * P], U8, name="w_plane", align_bytes=64)
         xb = [keep.tile([P, G, T, L], U8, name="xbytes%d" % i) for i in range(4)]
-        codes = [[keep.tile([P, R * Q], I32, name="codes%d_%d" % (s, g), align_bytes=64) for g in range(G)] for s in range(2)]
-        xcodes = [[keep.tile([P, 2 * PITCHW], I32, name="xcodes%d_%d" % (s, g), align_bytes=64) for g in range(G)] for s in range(2)]
+        codes = [keep.tile([P, G, R * Q], I32, name="codes%d" % s, align_bytes=64) for s in range(2)]
+        xcodes = [keep.tile([P, G, 2 * Q], I32, name="xcodes%d" % s, align_bytes=64) for s in range(2)]
         plane = [keep.tile([P, R * Q], U8, name="plane%d" % s, align_bytes=64) for s in range(2)]
         xplane = [keep.tile([P, 2 * PITCHB], U8, name="xplane%d" % s, align_bytes=64) for s in range(2)]
 
@@ -91,14 +91,9 @@ def tile_timeawareconv1d_t_kernel(tc, x_bytes, x_scale, time_tensor, weights, ou
         for s in range(2):
             nc.vector.memset(plane[s][:].bitcast(I32), 0)
             nc.vector.memset(xplane[s][:].bitcast(I32), 0)
-            for g in range(G):
-                nc.vector.memset(xcodes[s][g][:], 0)
-
-        if MANUAL:
-            ctx.enter_context(tc.manual_schedule(engines={mybir.EngineType.Activation, mybir.EngineType.DVE}))
+            nc.vector.memset(xcodes[s][:], 0)
 
         def transpose_weights(c):
-            tiles = []
             wg = gqpool.tile([P, KW * G * 512], BF16, name="wg", tag="gq", align_bytes=64)
             for j in range(KW):
                 for g in range(G):
@@ -144,37 +139,43 @@ def tile_timeawareconv1d_t_kernel(tc, x_bytes, x_scale, time_tensor, weights, ou
                 tiles.append(gq)
             return tiles
 
-        def quantise(s, g, gqs, q0, nq):
-            a, n = R * q0, R * nq
-            if g == 0:
-                nc.vector.quantize_mx(out=codes[s][0][:, a:a + n].bitcast(FP8X4), scales=plane[s][:, a:a + n], in_=gqs[0][:])
-            else:
-                step = min(n, 512)
-                for h in range(0, n, step):
-                    nc.vector.quantize_mx(out=codes[s][1][:, a + h:a + h + step].bitcast(FP8X4),
-                                          scales=plane[s][4:P, a + h:a + h + step],
-                                          in_=gqs[1][:, T * h:T * (h + step)])
+        def quantise(s, g, gq, q0, nq):
+            for a, d, n in ((0, C0 + q0, nq), (nq, C12 + 2 * q0, 2 * nq), (3 * nq, C3 + q0, nq)):
+                nc.vector.quantize_mx(out=codes[s][:, g, d:d + n].bitcast(FP8X4),
+                                      scales=plane[s][4 * g:P, d:d + n],
+                                      in_=gq[:, T * a:T * (a + n)])
 
-        def shift(s, q0, nq):
-            for g in range(G):
-                nc.vector.tensor_copy(
-                    out=xcodes[s][g][:].rearrange("p (e w) -> p e w", e=2)[:, :, PADW + q0 - 1:PADW + q0 - 1 + nq],
-                    in_=codes[s][g][:, R * q0:R * (q0 + nq)].rearrange("p (r q) -> p r q", r=R)[:, 0:R:R - 1, :])
+        def shift_codes(s, q0, nq, by_dma):
+            moves = []
+            lo, hi = max(q0 - WIN, 0), (q0 + nq - WIN if q0 + nq < Q else Q - 1)
+            if hi > lo:
+                moves.append((E4W + lo, C0 + lo + 1, hi - lo))
+            lo = max(q0, 1)
+            moves.append((EM1W + lo, C3 + lo - 1, q0 + nq - lo))
+            for d, a, n in moves:
+                if by_dma:
+                    nc.sync.dma_start(out=xcodes[s][:, :, d:d + n], in_=codes[s][:, :, a:a + n])
+                else:
+                    nc.vector.tensor_copy(out=xcodes[s][:, :, d:d + n], in_=codes[s][:, :, a:a + n])
+
+        def shift_plane(s, q0, nq):
             nc.vector.tensor_copy(
                 out=xplane[s][:].rearrange("p (e w) -> p e w", e=2)[:, :, PADB + q0 - 1:PADB + q0 - 1 + nq],
-                in_=plane[s][:, R * q0:R * (q0 + nq)].rearrange("p (r q) -> p r q", r=R)[:, 0:R:R - 1, :])
+                in_=plane[s][:, 0:2 * Q].rearrange("p (e q) -> p e q", e=2)[:, :, q0:q0 + nq])
 
         def operand(row, s, g, cls, w):
             k = 4 * g
+            a = WIN * w
             if cls < 0:
-                return (xcodes[s][g][:, EM1W + WIN * w:EM1W + WIN * (w + 1)], xplane[s][k:P, EM1B + WIN * w:EM1B + WIN * (w + 1)])
+                return (xcodes[s][:, g, EM1W + a:EM1W + a + WIN], xplane[s][k:P, EM1B + a:EM1B + a + WIN])
             if cls >= R:
-                return (xcodes[s][g][:, E4W + WIN * w:E4W + WIN * (w + 1)], xplane[s][k:P, E4B + WIN * w:E4B + WIN * (w + 1)])
-            for q0, nq in PIECES[row]:
-                if q0 <= WIN * w < q0 + nq:
-                    a = R * q0 + cls * nq + WIN * w - q0
-                    return (codes[s][g][:, a:a + WIN], plane[s][k:P, a:a + WIN])
-            raise ValueError("no piece")
+                return (xcodes[s][:, g, E4W + a:E4W + a + WIN], xplane[s][k:P, E4B + a:E4B + a + WIN])
+            if cls == 0 or cls == 3:
+                a += C0 if cls == 0 else C3
+            else:
+                q0, nq = [piece for piece in PIECES[row] if piece[0] <= a < piece[0] + piece[1]][0]
+                a += C12 + q0 + (cls - 1) * nq
+            return (codes[s][:, g, a:a + WIN], plane[s][k:P, a:a + WIN])
 
         banks = {}
 
@@ -215,20 +216,31 @@ def tile_timeawareconv1d_t_kernel(tc, x_bytes, x_scale, time_tensor, weights, ou
         backlog = []
         wg = None
         for n, (row, q0, nq) in enumerate(flat):
+            s = row % 2
             gqs = interleave(wds[n], nq, S_SHARE_TAIL if n + 2 > last else S_SHARE)
             if n < last:
                 wds[n + 1] = widen(n + 1, *flat[n + 1])
             if n in w_steps:
                 wg = transpose_weights(w_steps[n])
-            quantise(row % 2, 0, gqs, q0, nq)
-            for item in pending[:1]:
+            quantise(s, 0, gqs[0], q0, nq)
+            if n < last:
+                for item in pending[:1]:
+                    finish(*item)
+                pending = pending[1:]
+            quantise(s, 1, gqs[1], q0, nq)
+            by_dma = n + V_SHIFTS <= last
+            if by_dma:
+                shift_codes(s, q0, nq, True)
+            for item in pending[:1] if n == last else pending:
                 finish(*item)
-            quantise(row % 2, 1, gqs, q0, nq)
-            for item in pending[1:]:
-                finish(*item)
+            late = pending[1:] if n == last else []
             if n in w_steps:
                 quantise_weights(w_steps[n], wg)
-            shift(row % 2, q0, nq)
+            if not by_dma:
+                shift_codes(s, q0, nq, False)
+            shift_plane(s, q0, nq)
+            for item in late:
+                finish(*item)
             w0, w1 = q0 // WIN, (q0 + nq) // WIN
             whole = w1 * WIN == Q
             for w in range(w0, w1):

@@ -47,8 +47,7 @@ def tile_timeawareconv1d_t_kernel(tc, x_bytes, x_scale, time_tensor, weights, ou
         wdpool = ctx.enter_context(tc.tile_pool(name="wdpool", bufs=5))
         gqpool = ctx.enter_context(tc.tile_pool(name="gqpool", bufs=3))
         opool = ctx.enter_context(tc.tile_pool(name="opool", bufs=4))
-        pwpool = ctx.enter_context(tc.psum_pool(name="pwpool", bufs=2))
-        popool = ctx.enter_context(tc.psum_pool(name="popool", bufs=6))
+        popool = ctx.enter_context(tc.psum_pool(name="popool", bufs=8))
 
         ident = keep.tile([P, P], BF16, name="ident")
         make_identity(nc, ident[:])
@@ -98,7 +97,7 @@ def tile_timeawareconv1d_t_kernel(tc, x_bytes, x_scale, time_tensor, weights, ou
             for j in range(KW):
                 for g in range(G):
                     k = j * G + g
-                    pw = pwpool.tile([P, T, P], BF16, name="pw", tag="pw")
+                    pw = popool.tile([P, T, P], BF16, name="pw", tag="po")
                     view = w_raw[g][:].rearrange("o (p t c j) -> o p t c j", p=P, t=T, c=C, j=KW)
                     for t in range(T):
                         nc.tensor.transpose(out=pw[:, t, :], in_=view[:, :, t, c, j], identity=ident[:])
@@ -212,7 +211,7 @@ def tile_timeawareconv1d_t_kernel(tc, x_bytes, x_scale, time_tensor, weights, ou
         last = len(flat) - 1
         w_steps = {2: 0, 4: 1}
         wds = {0: widen(0, *flat[0])}
-        pending = []
+        closed = {}
         backlog = []
         wg = None
         for n, (row, q0, nq) in enumerate(flat):
@@ -222,25 +221,25 @@ def tile_timeawareconv1d_t_kernel(tc, x_bytes, x_scale, time_tensor, weights, ou
                 wds[n + 1] = widen(n + 1, *flat[n + 1])
             if n in w_steps:
                 wg = transpose_weights(w_steps[n])
+            due = closed.get(n - 2, []) + (closed.get(n - 1, []) if n == last else [])
             quantise(s, 0, gqs[0], q0, nq)
-            if n < last:
-                for item in pending[:1]:
-                    finish(*item)
-                pending = pending[1:]
+            for item in due[:1]:
+                finish(*item)
             quantise(s, 1, gqs[1], q0, nq)
             by_dma = n + V_SHIFTS <= last
             if by_dma:
                 shift_codes(s, q0, nq, True)
-            for item in pending[:1] if n == last else pending:
-                finish(*item)
-            late = pending[1:] if n == last else []
+            if n < last:
+                for item in due[1:]:
+                    finish(*item)
             if n in w_steps:
                 quantise_weights(w_steps[n], wg)
             if not by_dma:
                 shift_codes(s, q0, nq, False)
             shift_plane(s, q0, nq)
-            for item in late:
-                finish(*item)
+            if n == last:
+                for item in due[1:]:
+                    finish(*item)
             w0, w1 = q0 // WIN, (q0 + nq) // WIN
             whole = w1 * WIN == Q
             for w in range(w0, w1):
@@ -252,12 +251,12 @@ def tile_timeawareconv1d_t_kernel(tc, x_bytes, x_scale, time_tensor, weights, ou
                     backlog.append((row, w, (0, 3), True))
                 else:
                     backlog.append((row, w, (0,), False))
-            pending = []
+            closed[n] = []
             if n >= 2:
                 for brow, bw, classes, closes in backlog:
                     multiply(brow, bw, classes)
                     if closes:
-                        pending.append((brow, bw))
+                        closed[n].append((brow, bw))
                 backlog = []
-        for item in pending:
+        for item in closed[last]:
             finish(*item)

@@ -35,7 +35,7 @@ PIECES = [
     [(0, 256), (256, 128), (384, 128)],
 ]
 V_WIDENS = ((0, 1), (1, 1), (2, 1))
-S_SHARE = 1 / 16
+S_SHARE = 0
 S_SHARE_TAIL = 1 / 4
 V_SHIFTS = 2
 

@@ -34,9 +34,11 @@ PIECES = [
     [(0, 256), (256, 256)],
     [(0, 256), (256, 128), (384, 128)],
 ]
+LAST = sum(len(pieces) for pieces in PIECES) - 1
 V_WIDENS = ((0, 1), (1, 1), (2, 1))
 S_SHARE = 0
 S_SHARE_TAIL = 1 / 4
+WARM = 256
 V_SHIFTS = 2
 
 
@@ -90,7 +92,7 @@ def tile_timeawareconv1d_t_kernel(tc, x_bytes, x_scale, time_tensor, weights, ou
         for s in range(2):
             nc.vector.memset(plane[s][:].bitcast(I32), 0)
             nc.vector.memset(xplane[s][:].bitcast(I32), 0)
-            nc.vector.memset(xcodes[s][:], 0)
+            nc.vector.memset(xcodes[s][:, :, Q - 8:Q + 8], 0)
 
         def transpose_weights(c):
             wg = gqpool.tile([P, KW * G * 512], BF16, name="wg", tag="gq", align_bytes=64)
@@ -112,6 +114,10 @@ def tile_timeawareconv1d_t_kernel(tc, x_bytes, x_scale, time_tensor, weights, ou
                                       scales=w_plane[:, base + a:base + a + n],
                                       in_=wg[:, 4 * a:4 * (a + n)])
 
+        def keep_warm(rows):
+            scratch = popool.tile([P, WARM], F32, name="scratch", tag="po")
+            nc.tensor.matmul(out=scratch[:], lhsT=ident[:], rhs=rows, start=True, stop=True)
+
         def widen(n, row, q0, nq):
             tiles = []
             for g in range(G):
@@ -122,10 +128,12 @@ def tile_timeawareconv1d_t_kernel(tc, x_bytes, x_scale, time_tensor, weights, ou
                         nc.vector.tensor_scalar(out=wd[:, t, :], in0=src, scalar1=sc[:, g, t:t + 1], scalar2=None, op0=MULT)
                     else:
                         nc.scalar.activation(out=wd[:, t, :], in_=src, func=COPY, scale=sc[:, g, t:t + 1])
+                    if n == LAST:
+                        keep_warm(wd[:, t, 0:WARM])
                 tiles.append(wd)
             return tiles
 
-        def interleave(wds, nq, share):
+        def interleave(wds, nq, share, warm):
             tiles = []
             cut = nq - 4 * int(nq * share / 4)
             for g in range(G):
@@ -135,6 +143,8 @@ def tile_timeawareconv1d_t_kernel(tc, x_bytes, x_scale, time_tensor, weights, ou
                 if cut < nq:
                     nc.scalar.copy(out=dst[:, cut:nq], in_=src[:, cut:nq])
                 nc.vector.tensor_copy(out=dst[:, 0:cut], in_=src[:, 0:cut])
+                if warm:
+                    keep_warm(gq[:, 0:WARM])
                 tiles.append(gq)
             return tiles
 
@@ -216,7 +226,7 @@ def tile_timeawareconv1d_t_kernel(tc, x_bytes, x_scale, time_tensor, weights, ou
         wg = None
         for n, (row, q0, nq) in enumerate(flat):
             s = row % 2
-            gqs = interleave(wds[n], nq, S_SHARE_TAIL if n + 2 > last else S_SHARE)
+            gqs = interleave(wds[n], nq, S_SHARE_TAIL if n + 2 > last else S_SHARE, n == last)
             if n < last:
                 wds[n + 1] = widen(n + 1, *flat[n + 1])
             if n in w_steps:

@@ -54,6 +54,9 @@ def tile_timeawareconv1d_t_kernel(tc, x_bytes, x_scale, time_tensor, weights, ou
         ident = keep.tile([P, P], BF16, name="ident")
         make_identity(nc, ident[:])
         sc = keep.tile([P, G, T], F32, name="sc")
+        first = keep.tile([P, 2], F32, name="first")
+        nc.vector.memset(first[:, 0:1], 0.0)
+        nc.scalar.activation(out=first[:, 1:2], in_=first[:, 0:1], func=COPY, scale=1.0)
         tt = keep.tile([P, B * C * L], BF16, name="tt")
         w_raw = [keep.tile([P, 512 * C * KW], BF16, name="w_raw%d" % g) for g in range(G)]
         w_codes = keep.tile([P, C * KW * G * P], I32, name="w_codes", align_bytes=64)

@@ -67,18 +67,21 @@ def tile_timeawareconv1d_t_kernel(tc, x_bytes, x_scale, time_tensor, weights, ou
         plane = [keep.tile([P, R * Q], U8, name="plane%d" % s, align_bytes=64) for s in range(2)]
         xplane = [keep.tile([P, 2 * PITCHB], U8, name="xplane%d" % s, align_bytes=64) for s in range(2)]
 
-        def load_x(row, g, l0, l1):
+        def load_x(row, g, l0, l1, t0=0, t1=T):
             b, c = ROWS[row]
             src = x_bytes[b].rearrange("(g p t) c l -> g p t c l", g=G, p=P, t=T)
-            nc.sync.dma_start(out=xb[row][:, g, :, l0:l1], in_=src[g][:, :, c, l0:l1])
+            nc.sync.dma_start(out=xb[row][:, g, t0:t1, l0:l1], in_=src[g][:, t0:t1, c, l0:l1])
 
         def load_time(row):
             b, c = ROWS[row]
             t0 = (b * C + c) * L
             nc.sync.dma_start(out=tt[:, t0:t0 + L], in_=time_tensor[b, c].partition_broadcast(P))
 
-        nc.sync.dma_start(out=sc[:], in_=x_scale.rearrange("o (g p t) a b -> p (o g) (t a b)", g=G, p=P, t=T))
-        for q0, nq in PIECES[0]:
+        nc.scalar.dma_start(out=sc[:], in_=x_scale.rearrange("o (g p t) a b -> p (o g) (t a b)", g=G, p=P, t=T))
+        for t0, t1 in ((0, 1), (1, T)):
+            for g in range(G):
+                load_x(0, g, 0, R * PIECES[0][0][1], t0, t1)
+        for q0, nq in PIECES[0][1:]:
             for g in range(G):
                 load_x(0, g, R * q0, R * (q0 + nq))
         for g in range(G):
@@ -191,23 +194,19 @@ def tile_timeawareconv1d_t_kernel(tc, x_bytes, x_scale, time_tensor, weights, ou
 
         banks = {}
 
-        def multiply(row, w, classes):
+        def multiply(row, w, r, passes, opens, closes):
             b, c = ROWS[row]
             s = row % 2
             if (row, w) not in banks:
                 banks[(row, w)] = popool.tile([P, R * WIN], F32, name="po", tag="po")
             po = banks[(row, w)]
-            for r in classes:
-                k = 0
-                for g in range(G):
-                    for j in range(KW):
-                        rhs, rhs_scale = operand(row, s, g, r + j - 1, w)
-                        a = ((c * KW + j) * G + g) * P
-                        nc.tensor.matmul_mx(out=po[:, r * WIN:(r + 1) * WIN],
-                                            lhsT=w_codes[:, a:a + P].bitcast(FP8X4), lhsT_scale=w_plane[:, a:a + P],
-                                            rhs=rhs.bitcast(FP8X4), rhs_scale=rhs_scale,
-                                            start=(k == 0), stop=(k == G * KW - 1))
-                        k += 1
+            for k, (g, j) in enumerate(passes):
+                rhs, rhs_scale = operand(row, s, g, r + j - 1, w)
+                a = ((c * KW + j) * G + g) * P
+                nc.tensor.matmul_mx(out=po[:, r * WIN:(r + 1) * WIN],
+                                    lhsT=w_codes[:, a:a + P].bitcast(FP8X4), lhsT_scale=w_plane[:, a:a + P],
+                                    rhs=rhs.bitcast(FP8X4), rhs_scale=rhs_scale,
+                                    start=(opens and k == 0), stop=(closes and k == len(passes) - 1))
 
         def finish(row, w):
             b, c = ROWS[row]
@@ -255,20 +254,23 @@ def tile_timeawareconv1d_t_kernel(tc, x_bytes, x_scale, time_tensor, weights, ou
                     finish(*item)
             w0, w1 = q0 // WIN, (q0 + nq) // WIN
             whole = w1 * WIN == Q
+            every = [(g, j) for g in range(G) for j in range(KW)]
             for w in range(w0, w1):
-                backlog.append((row, w, (1, 2), False))
+                backlog.append((row, w, 1, every, True, True, False))
+                backlog.append((row, w, 2, every, True, True, False))
             if w0 > 0:
-                backlog.append((row, w0 - 1, (3,), True))
+                backlog.append((row, w0 - 1, 3, [(g, 2) for g in range(G)], False, True, True))
             for w in range(w0, w1):
+                backlog.append((row, w, 0, every, True, True, False))
                 if w + 1 < w1 or whole:
-                    backlog.append((row, w, (0, 3), True))
+                    backlog.append((row, w, 3, every, True, True, True))
                 else:
-                    backlog.append((row, w, (0,), False))
+                    backlog.append((row, w, 3, [(g, j) for g in range(G) for j in range(2)], True, False, False))
             closed[n] = []
             if n >= 2:
-                for brow, bw, classes, closes in backlog:
-                    multiply(brow, bw, classes)
-                    if closes:
+                for brow, bw, r, passes, opens, closes, is_last in backlog:
+                    multiply(brow, bw, r, passes, opens, closes)
+                    if is_last:
                         closed[n].append((brow, bw))
                 backlog = []
         for item in closed[last]:

@@ -36,6 +36,7 @@ PIECES = [
 ]
 LAST = sum(len(pieces) for pieces in PIECES) - 1
 V_WIDENS = ((0, 1), (1, 1), (2, 1))
+S_ROWS = ((2, 1, 0),)
 S_SHARE = 0
 S_SHARE_TAIL = 1 / 4
 WARM = 256
@@ -130,7 +131,7 @@ def tile_timeawareconv1d_t_kernel(tc, x_bytes, x_scale, time_tensor, weights, ou
                 wd = wdpool.tile([P, T, R * nq], BF16, name="wd", tag="wd")
                 for t in range(T):
                     src = xb[row][:, g, t, R * q0:R * (q0 + nq)].bitcast(FP8)
-                    if (n, g) in V_WIDENS:
+                    if (n, g) in V_WIDENS and (n, g, t) not in S_ROWS:
                         nc.vector.tensor_scalar(out=wd[:, t, :], in0=src, scalar1=sc[:, g, t:t + 1], scalar2=None, op0=MULT)
                     else:
                         nc.scalar.activation(out=wd[:, t, :], in_=src, func=COPY, scale=sc[:, g, t:t + 1])

@@ -39,7 +39,6 @@ V_WIDENS = ((0, 1), (1, 1), (2, 1))
 S_ROWS = ((2, 1, 0),)
 S_SHARE = 0
 S_SHARE_TAIL = 1 / 4
-WARM = 256
 V_SHIFTS = 2
 
 
@@ -121,10 +120,6 @@ def tile_timeawareconv1d_t_kernel(tc, x_bytes, x_scale, time_tensor, weights, ou
                                       scales=w_plane[:, base + a:base + a + n],
                                       in_=wg[:, 4 * a:4 * (a + n)])
 
-        def keep_warm(rows):
-            scratch = popool.tile([P, WARM], F32, name="scratch", tag="po")
-            nc.tensor.matmul(out=scratch[:], lhsT=ident[:], rhs=rows, start=True, stop=True)
-
         def widen(n, row, q0, nq):
             tiles = []
             for g in range(G):
@@ -135,12 +130,10 @@ def tile_timeawareconv1d_t_kernel(tc, x_bytes, x_scale, time_tensor, weights, ou
                         nc.vector.tensor_scalar(out=wd[:, t, :], in0=src, scalar1=sc[:, g, t:t + 1], scalar2=None, op0=MULT)
                     else:
                         nc.scalar.activation(out=wd[:, t, :], in_=src, func=COPY, scale=sc[:, g, t:t + 1])
-                    if n == LAST:
-                        keep_warm(wd[:, t, 0:WARM])
                 tiles.append(wd)
             return tiles
 
-        def interleave(wds, nq, share, warm):
+        def interleave(wds, nq, share):
             tiles = []
             cut = nq - 4 * int(nq * share / 4)
             for g in range(G):
@@ -150,8 +143,6 @@ def tile_timeawareconv1d_t_kernel(tc, x_bytes, x_scale, time_tensor, weights, ou
                 if cut < nq:
                     nc.scalar.copy(out=dst[:, cut:nq], in_=src[:, cut:nq])
                 nc.vector.tensor_copy(out=dst[:, 0:cut], in_=src[:, 0:cut])
-                if warm:
-                    keep_warm(gq[:, 0:WARM])
                 tiles.append(gq)
             return tiles
 
@@ -229,7 +220,7 @@ def tile_timeawareconv1d_t_kernel(tc, x_bytes, x_scale, time_tensor, weights, ou
         wg = None
         for n, (row, q0, nq) in enumerate(flat):
             s = row % 2
-            gqs = interleave(wds[n], nq, S_SHARE_TAIL if n + 2 > last else S_SHARE, n == last)
+            gqs = interleave(wds[n], nq, S_SHARE_TAIL if n + 2 > last else S_SHARE)
             if n < last:
                 wds[n + 1] = widen(n + 1, *flat[n + 1])
             if n in w_steps:

@@ -85,9 +85,11 @@ def tile_timeawareconv1d_t_kernel(tc, x_bytes, x_scale, time_tensor, weights, ou
             for g in range(G):
                 load_x(0, g, R * q0, R * (q0 + nq))
         for g in range(G):
-            load_x(1, g, 0, L)
+            load_x(1, g, 0, L // 2)
         for g in range(G):
             nc.sync.dma_start(out=w_raw[g][:], in_=weights[:, g * 512:(g + 1) * 512, :, :].rearrange("o i c j -> o (i c j)"))
+        for g in range(G):
+            load_x(1, g, L // 2, L)
         load_time(0)
         for row in range(2, 4):
             for g in range(G):

from contextlib import ExitStack

import concourse.mybir as mybir
from concourse.masks import make_identity

B, I, C, L, O, KW = 2, 1024, 2, 2048, 128, 3
FLOPS = 2 * B * C * O * I * KW * L

F32 = mybir.dt.float32
BF16 = mybir.dt.bfloat16
I32 = mybir.dt.int32
U8 = mybir.dt.uint8
FP8 = mybir.dt.float8_e4m3fn
FP8X4 = mybir.dt.float8_e4m3fn_x4
COPY = mybir.ActivationFunctionType.Copy
MULT = mybir.AluOpType.mult

P = 128
G = 2
T = 4
R = 4
Q = L // R
WIN = 128

C0, C3, C12 = 0, Q, 2 * Q
E4W, EM1W = 0, Q
PADB, PITCHB = 64, 642
E4B, EM1B = PADB, PITCHB + PADB - 2

ROWS = [(0, 0), (1, 0), (0, 1), (1, 1)]
PIECES = [
    [(0, 128), (128, 128), (256, 256)],
    [(0, 256), (256, 256)],
    [(0, 256), (256, 256)],
    [(0, 256), (256, 128), (384, 128)],
]
LAST = sum(len(pieces) for pieces in PIECES) - 1
V_WIDENS = ((0, 1), (1, 1), (2, 1))
S_ROWS = ((2, 1, 0),)
S_SHARE = 0
S_SHARE_TAIL = 1 / 4
V_SHIFTS = 2


def tile_timeawareconv1d_t_kernel(tc, x_bytes, x_scale, time_tensor, weights, out):
    nc = tc.nc
    with ExitStack() as ctx:
        keep = ctx.enter_context(tc.tile_pool(name="keep", bufs=1))
        wdpool = ctx.enter_context(tc.tile_pool(name="wdpool", bufs=5))
        gqpool = ctx.enter_context(tc.tile_pool(name="gqpool", bufs=3))
        opool = ctx.enter_context(tc.tile_pool(name="opool", bufs=4))
        popool = ctx.enter_context(tc.psum_pool(name="popool", bufs=8))

        ident = keep.tile([P, P], BF16, name="ident")
        make_identity(nc, ident[:])
        sc = keep.tile([P, G, T], F32, name="sc")
        first = keep.tile([P, 2], F32, name="first")
        nc.vector.memset(first[:, 0:1], 0.0)
        nc.scalar.activation(out=first[:, 1:2], in_=first[:, 0:1], func=COPY, scale=1.0)
        tt = keep.tile([P, B * C * L], BF16, name="tt")
        w_raw = [keep.tile([P, 512 * C * KW], BF16, name="w_raw%d" % g) for g in range(G)]
        w_codes = keep.tile([P, C * KW * G * P], I32, name="w_codes", align_bytes=64)
        w_plane = keep.tile([P, C * KW * G * P], U8, name="w_plane", align_bytes=64)
        xb = [keep.tile([P, G, T, L], U8, name="xbytes%d" % i) for i in range(4)]
        codes = [keep.tile([P, G, R * Q], I32, name="codes%d" % s, align_bytes=64) for s in range(2)]
        xcodes = [keep.tile([P, G, 2 * Q], I32, name="xcodes%d" % s, align_bytes=64) for s in range(2)]
        plane = [keep.tile([P, R * Q], U8, name="plane%d" % s, align_bytes=64) for s in range(2)]
        xplane = [keep.tile([P, 2 * PITCHB], U8, name="xplane%d" % s, align_bytes=64) for s in range(2)]

        def load_x(row, g, l0, l1, t0=0, t1=T):
            b, c = ROWS[row]
            src = x_bytes[b].rearrange("(g p t) c l -> g p t c l", g=G, p=P, t=T)
            nc.sync.dma_start(out=xb[row][:, g, t0:t1, l0:l1], in_=src[g][:, t0:t1, c, l0:l1])

        def load_time(row):
            b, c = ROWS[row]
            t0 = (b * C + c) * L
            nc.sync.dma_start(out=tt[:, t0:t0 + L], in_=time_tensor[b, c].partition_broadcast(P))

        nc.scalar.dma_start(out=sc[:], in_=x_scale.rearrange("o (g p t) a b -> p (o g) (t a b)", g=G, p=P, t=T))
        for t0, t1 in ((0, 1), (1, T)):
            for g in range(G):
                load_x(0, g, 0, R * PIECES[0][0][1], t0, t1)
        for q0, nq in PIECES[0][1:]:
            for g in range(G):
                load_x(0, g, R * q0, R * (q0 + nq))
        for g in range(G):
            load_x(1, g, 0, L // 2)
        for g in range(G):
            nc.sync.dma_start(out=w_raw[g][:], in_=weights[:, g * 512:(g + 1) * 512, :, :].rearrange("o i c j -> o (i c j)"))
        for g in range(G):
            load_x(1, g, L // 2, L)
        load_time(0)
        for row in range(2, 4):
            for g in range(G):
                load_x(row, g, 0, L)
            load_time(row - 1)
        load_time(3)

        for s in range(2):
            nc.vector.memset(plane[s][:].bitcast(I32), 0)
            nc.vector.memset(xplane[s][:].bitcast(I32), 0)
            nc.vector.memset(xcodes[s][:, :, Q - 8:Q + 8], 0)

        def transpose_weights(c):
            wg = gqpool.tile([P, KW * G * 512], BF16, name="wg", tag="gq", align_bytes=64)
            for j in range(KW):
                for g in range(G):
                    k = j * G + g
                    pw = popool.tile([P, T, P], BF16, name="pw", tag="po")
                    view = w_raw[g][:].rearrange("o (p t c j) -> o p t c j", p=P, t=T, c=C, j=KW)
                    for t in range(T):
                        nc.tensor.transpose(out=pw[:, t, :], in_=view[:, :, t, c, j], identity=ident[:])
                    nc.scalar.copy(out=wg[:, k * 512:(k + 1) * 512].rearrange("p (o t) -> p o t", t=T),
                                   in_=pw[:].rearrange("p t o -> p o t"))
            return wg

        def quantise_weights(c, wg):
            base = c * KW * G * P
            for a, n in ((0, 512), (512, 256)):
                nc.vector.quantize_mx(out=w_codes[:, base + a:base + a + n].bitcast(FP8X4),
                                      scales=w_plane[:, base + a:base + a + n],
                                      in_=wg[:, 4 * a:4 * (a + n)])

        def widen(n, row, q0, nq):
            tiles = []
            for g in range(G):
                wd = wdpool.tile([P, T, R * nq], BF16, name="wd", tag="wd")
                for t in range(T):
                    src = xb[row][:, g, t, R * q0:R * (q0 + nq)].bitcast(FP8)
                    if (n, g) in V_WIDENS and (n, g, t) not in S_ROWS:
                        nc.vector.tensor_scalar(out=wd[:, t, :], in0=src, scalar1=sc[:, g, t:t + 1], scalar2=None, op0=MULT)
                    else:
                        nc.scalar.activation(out=wd[:, t, :], in_=src, func=COPY, scale=sc[:, g, t:t + 1])
                tiles.append(wd)
            return tiles

        def interleave(wds, nq, share):
            tiles = []
            cut = nq - 4 * int(nq * share / 4)
            for g in range(G):
                gq = gqpool.tile([P, R * nq * T], BF16, name="gq", tag="gq", align_bytes=64)
                dst = gq[:].rearrange("p (r q t) -> p q t r", r=R, t=T)
                src = wds[g][:].rearrange("p t (q r) -> p q t r", r=R)
                if cut < nq:
                    nc.scalar.copy(out=dst[:, cut:nq], in_=src[:, cut:nq])
                nc.vector.tensor_copy(out=dst[:, 0:cut], in_=src[:, 0:cut])
                tiles.append(gq)
            return tiles

        def quantise(s, g, gq, q0, nq):
            for a, d, n in ((0, C0 + q0, nq), (nq, C12 + 2 * q0, 2 * nq), (3 * nq, C3 + q0, nq)):
                nc.vector.quantize_mx(out=codes[s][:, g, d:d + n].bitcast(FP8X4),
                                      scales=plane[s][4 * g:P, d:d + n],
                                      in_=gq[:, T * a:T * (a + n)])

        def shift_codes(s, q0, nq, by_dma):
            moves = []
            lo, hi = max(q0 - WIN, 0), (q0 + nq - WIN if q0 + nq < Q else Q - 1)
            if hi > lo:
                moves.append((E4W + lo, C0 + lo + 1, hi - lo))
            lo = max(q0, 1)
            moves.append((EM1W + lo, C3 + lo - 1, q0 + nq - lo))
            for d, a, n in moves:
                if by_dma:
                    nc.sync.dma_start(out=xcodes[s][:, :, d:d + n], in_=codes[s][:, :, a:a + n])
                else:
                    nc.vector.tensor_copy(out=xcodes[s][:, :, d:d + n], in_=codes[s][:, :, a:a + n])

        def shift_plane(s, q0, nq):
            nc.vector.tensor_copy(
                out=xplane[s][:].rearrange("p (e w) -> p e w", e=2)[:, :, PADB + q0 - 1:PADB + q0 - 1 + nq],
                in_=plane[s][:, 0:2 * Q].rearrange("p (e q) -> p e q", e=2)[:, :, q0:q0 + nq])

        def operand(row, s, g, cls, w):
            k = 4 * g
            a = WIN * w
            if cls < 0:
                return (xcodes[s][:, g, EM1W + a:EM1W + a + WIN], xplane[s][k:P, EM1B + a:EM1B + a + WIN])
            if cls >= R:
                return (xcodes[s][:, g, E4W + a:E4W + a + WIN], xplane[s][k:P, E4B + a:E4B + a + WIN])
            if cls == 0 or cls == 3:
                a += C0 if cls == 0 else C3
            else:
                q0, nq = [piece for piece in PIECES[row] if piece[0] <= a < piece[0] + piece[1]][0]
                a += C12 + q0 + (cls - 1) * nq
            return (codes[s][:, g, a:a + WIN], plane[s][k:P, a:a + WIN])

        banks = {}

        def multiply(row, w, r, passes, opens, closes):
            b, c = ROWS[row]
            s = row % 2
            if (row, w) not in banks:
                banks[(row, w)] = popool.tile([P, R * WIN], F32, name="po", tag="po")
            po = banks[(row, w)]
            for k, (g, j) in enumerate(passes):
                rhs, rhs_scale = operand(row, s, g, r + j - 1, w)
                a = ((c * KW + j) * G + g) * P
                nc.tensor.matmul_mx(out=po[:, r * WIN:(r + 1) * WIN],
                                    lhsT=w_codes[:, a:a + P].bitcast(FP8X4), lhsT_scale=w_plane[:, a:a + P],
                                    rhs=rhs.bitcast(FP8X4), rhs_scale=rhs_scale,
                                    start=(opens and k == 0), stop=(closes and k == len(passes) - 1))

        def finish(row, w):
            b, c = ROWS[row]
            po = banks[(row, w)]
            l0 = R * WIN * w
            t0 = (b * C + c) * L + l0
            osb = opool.tile([P, R * WIN], F32, name="osb", tag="osb")
            nc.vector.tensor_tensor(out=osb[:].rearrange("p (q r) -> p q r", r=R),
                                    in0=po[:].rearrange("p (r q) -> p q r", r=R),
                                    in1=tt[:, t0:t0 + R * WIN].rearrange("p (q r) -> p q r", r=R), op=MULT)
            nc.sync.dma_start(out=out[b, :, c, l0:l0 + R * WIN], in_=osb[:])

        flat = [(row, q0, nq) for row in range(4) for (q0, nq) in PIECES[row]]
        last = len(flat) - 1
        w_steps = {2: 0, 4: 1}
        wds = {0: widen(0, *flat[0])}
        closed = {}
        backlog = []
        wg = None
        for n, (row, q0, nq) in enumerate(flat):
            s = row % 2
            gqs = interleave(wds[n], nq, S_SHARE_TAIL if n + 2 > last else S_SHARE)
            if n < last:
                wds[n + 1] = widen(n + 1, *flat[n + 1])
            if n in w_steps:
                wg = transpose_weights(w_steps[n])
            due = closed.get(n - 2, []) + (closed.get(n - 1, []) if n == last else [])
            quantise(s, 0, gqs[0], q0, nq)
            for item in due[:1]:
                finish(*item)
            quantise(s, 1, gqs[1], q0, nq)
            by_dma = n + V_SHIFTS <= last
            if by_dma:
                shift_codes(s, q0, nq, True)
            if n < last:
                for item in due[1:]:
                    finish(*item)
            if n in w_steps:
                quantise_weights(w_steps[n], wg)
            if not by_dma:
                shift_codes(s, q0, nq, False)
            shift_plane(s, q0, nq)
            if n == last:
                for item in due[1:]:
                    finish(*item)
            w0, w1 = q0 // WIN, (q0 + nq) // WIN
            whole = w1 * WIN == Q
            every = [(g, j) for g in range(G) for j in range(KW)]
            for w in range(w0, w1):
                backlog.append((row, w, 1, every, True, True, False))
                backlog.append((row, w, 2, every, True, True, False))
            if w0 > 0:
                backlog.append((row, w0 - 1, 3, [(g, 2) for g in range(G)], False, True, True))
            for w in range(w0, w1):
                backlog.append((row, w, 0, every, True, True, False))
                if w + 1 < w1 or whole:
                    backlog.append((row, w, 3, every, True, True, True))
                else:
                    backlog.append((row, w, 3, [(g, j) for g in range(G) for j in range(2)], True, False, False))
            closed[n] = []
            if n >= 2:
                for brow, bw, r, passes, opens, closes, is_last in backlog:
                    multiply(brow, bw, r, passes, opens, closes)
                    if is_last:
                        closed[n].append((brow, bw))
                backlog = []
        for item in closed[last]:
            finish(*item)
